import numpy as np
import ml_dtypes


def mxq(x, axis, fmt="e4m3"):
    dtype, down = {"e4m3": (ml_dtypes.float8_e4m3fn, 7), "e5m2": (ml_dtypes.float8_e5m2, 14)}[fmt]
    v = np.moveaxis(np.asarray(x, np.float32).astype(ml_dtypes.bfloat16).astype(np.float64), axis, -1)
    blocks = v.reshape(v.shape[:-1] + (-1, 32))
    amax = np.abs(blocks).max(-1, keepdims=True)
    byte = np.maximum(np.where(amax > 0, np.frexp(amax)[1] - 1 + 127, 0) - down, 1)
    scale = np.exp2(byte - 127.0)
    codes = (blocks / scale).astype(np.float32).astype(dtype).astype(np.float64)
    return np.moveaxis((codes * scale).reshape(v.shape), -1, axis)


WIDE = False


def mx_kscale(k):
    if not WIDE:
        return np.ones(k)
    levels = np.array([10, -10, 5, -5, 0])
    a = np.random.permutation(np.resize(levels, k // 512 * 4)).reshape(k // 512, 4)
    idx = np.arange(k)
    return np.exp2(a[idx // 512, idx % 128 // 32])


BF16 = ml_dtypes.bfloat16


def bf(x):
    return np.asarray(x, np.float32).astype(BF16)


def f64(x):
    return np.asarray(x).astype(np.float64)


B, N0, N1, N2, M0, M1, M2, QA, QB = 8, 16, 16, 16, 16, 8, 128, 8, 4
RA, RB = QA * QA, QB * QB
M = M0 * M1 * M2
T0 = B * M0
KA, KB = RA * M1, RB * M2
L = 1.0


def setup_inputs():
    s = mx_kscale(KA).reshape(RA, M1)
    d1 = np.random.standard_normal((RA, M1, M2, T0)) * 1.2 * s[:, :, None, None]
    g1 = np.random.standard_normal((RA, M1, M1, RB)) / np.sqrt(KA) / s[:, None, :, None]
    g2 = np.random.standard_normal((RB, M2, M2))[..., None] * 0.2 / np.sqrt(KB)
    return {'d1': bf(d1.reshape(RA, M1 * M2, T0)), 'g1': bf(g1), 'g2': bf(g2),
            'x_l': bf(np.random.standard_normal((B, M)) * 1.2), 'mv': bf(np.random.standard_normal((B, M))),
            'bias': bf(np.random.standard_normal(M) * 0.2)}


def reference(d1, g1, g2, x_l, mv, bias):
    a = f64(d1).reshape(KA, M2 * T0)
    w1 = f64(g1).transpose(0, 2, 3, 1).reshape(KA, RB * M1)
    y = mxq(a, 0, 'e4m3').T @ mxq(w1, 0, 'e4m3')
    d2 = y.reshape(M2, T0, RB, M1).transpose(2, 0, 1, 3).reshape(KB, T0 * M1)
    w2 = f64(g2).reshape(RB, M2, M2).transpose(0, 2, 1).reshape(KB, M2)
    term = (mxq(d2, 0, 'e4m3').T @ mxq(w2, 0, 'e4m3')).reshape(B, M)
    return f64(x_l) - term / L + f64(mv) / L + f64(bias)

@@ -1,0 +1,203 @@
+from contextlib import ExitStack
+
+import concourse.mybir as mybir
+from concourse.masks import make_identity
+
+BF16 = mybir.dt.bfloat16
+F32 = mybir.dt.float32
+U32 = mybir.dt.uint32
+U8 = mybir.dt.uint8
+FP8X4 = mybir.dt.float8_e4m3fn_x4
+
+P = 128
+PACK = 4
+A = 128
+T = 128
+M_OUT = 8
+RANK_B = 16
+J_OUT = 128
+ROW = M_OUT * J_OUT
+
+A_UNIT = 8
+UNITS = A // A_UNIT
+UNIT_COLS = A_UNIT * T
+A_BANK = 4
+RUN = 4
+VECTOR_COLS = 6 * T
+
+FLOPS = 2 * 512 * 128 * 16384 + 2 * 2048 * 1024 * 128
+
+
+def tile_ttsolver_pa_t_kernel(tc, d1, g1, g2, x_l, mv, bias, out):
+    nc = tc.nc
+
+    d1_rows = d1.rearrange("r (h j c) t -> (r h) j (c t)", h=2, j=PACK)
+    x_rows = x_l.rearrange("b (q c) -> (b q) c", c=ROW)
+    mv_rows = mv.rearrange("b (q c) -> (b q) c", c=ROW)
+    bias_rows = bias.rearrange("(q c) -> q c", c=ROW)
+    out_rows = out.rearrange("b (q c) -> (b q) c", c=ROW)
+
+    with ExitStack() as pools:
+        keep = pools.enter_context(tc.tile_pool(name="keep", bufs=1))
+        raw_pool = pools.enter_context(tc.tile_pool(name="raw", bufs=UNITS))
+        stage = pools.enter_context(tc.tile_pool(name="stage", bufs=2))
+        y_pool = pools.enter_context(tc.tile_pool(name="y_pool", bufs=3))
+        psum_y = pools.enter_context(tc.psum_pool(name="psum_y", bufs=4))
+        psum_t = pools.enter_context(tc.psum_pool(name="psum_t", bufs=1))
+
+        ident = keep.tile([P, P], BF16)
+        make_identity(nc, ident[:])
+
+        g1_raw = keep.tile([P, M_OUT, PACK * RANK_B], BF16)
+        for h in range(2):
+            nc.sync.dma_start(
+                out=g1_raw[h:P:2, :, :],
+                in_=g1[:, :, PACK * h : PACK * (h + 1), :].rearrange("r m j s -> r m (j s)"),
+            )
+        g2_raw = keep.tile([P, RANK_B, A], BF16)
+        nc.sync.dma_start(out=g2_raw[:], in_=g2.rearrange("s o a x -> o s (a x)"))
+        raw_tiles = []
+        for u in range(UNITS):
+            raw = raw_pool.tile([P, PACK, UNIT_COLS], BF16)
+            nc.sync.dma_start(out=raw[:], in_=d1_rows[:, :, u * UNIT_COLS : (u + 1) * UNIT_COLS])
+            raw_tiles.append(raw)
+        x_sb = keep.tile([P, ROW], BF16)
+        nc.sync.dma_start(out=x_sb[:], in_=x_rows)
+        mv_sb = keep.tile([P, ROW], BF16)
+        nc.sync.dma_start(out=mv_sb[:], in_=mv_rows)
+        bias_sb = keep.tile([P, ROW], BF16)
+        for b in range(P // 16):
+            nc.sync.dma_start(out=bias_sb[16 * b : 16 * (b + 1), :], in_=bias_rows)
+
+        w1_grouped = keep.tile([P, M_OUT, RANK_B, PACK], BF16, align_bytes=64)
+        nc.vector.tensor_copy(
+            out=w1_grouped[:], in_=g1_raw[:].rearrange("p m (j s) -> p m s j", j=PACK)
+        )
+        w1_codes = keep.tile([P, M_OUT * RANK_B], U32, align_bytes=64)
+        w1_scales = keep.tile([P, M_OUT * RANK_B], U8, align_bytes=64)
+        nc.vector.quantize_mx(
+            out=w1_codes[:].bitcast(FP8X4),
+            scales=w1_scales[:],
+            in_=w1_grouped[:].rearrange("p m s j -> p (m s j)"),
+        )
+
+        g2_sorted = keep.tile([P, A // A_UNIT, A_UNIT, RANK_B], BF16)
+        g2_view = g2_raw[:].rearrange("p s (c a) -> p c a s", a=A_UNIT)
+        nc.vector.tensor_copy(out=g2_sorted[:, 0:8, :, :], in_=g2_view[:, 0:8, :, :])
+        nc.scalar.copy(out=g2_sorted[:, 8:16, :, :], in_=g2_view[:, 8:16, :, :])
+        w2_grouped = keep.tile([P, PACK, J_OUT, PACK], BF16, align_bytes=64)
+        for pair in range(2):
+            w_ps = psum_t.tile([P, 2, PACK, J_OUT], BF16, tag="t_bank%d" % pair)
+            for c in range(8):
+                nc.tensor.transpose(
+                    w_ps[:, c // PACK, c % PACK, :],
+                    g2_sorted[:, 8 * pair + c, :, :].rearrange("p a s -> p (a s)"),
+                    ident[:],
+                )
+            nc.scalar.copy(
+                out=w2_grouped[:, 2 * pair : 2 * pair + 2, :, :],
+                in_=w_ps[:].rearrange("p g j o -> p g o j"),
+            )
+        w2_codes = keep.tile([P, PACK, J_OUT], U32, align_bytes=64)
+        w2_scales = keep.tile([P, PACK, J_OUT], U8, align_bytes=64)
+        nc.vector.quantize_mx(
+            out=w2_codes[:].rearrange("p g o -> p (g o)").bitcast(FP8X4),
+            scales=w2_scales[:].rearrange("p g o -> p (g o)"),
+            in_=w2_grouped[:].rearrange("p g o j -> p (g o j)"),
+        )
+
+        d2_codes = keep.tile([P, PACK, M_OUT * T], U32, align_bytes=64)
+        d2_scales = keep.tile([P, PACK, M_OUT * T], U8, align_bytes=64)
+        t_banks = []
+        for u in range(UNITS):
+            g, j = divmod(u, PACK)
+            raw = raw_tiles[u]
+            grouped = stage.tile([P, UNIT_COLS, PACK], BF16, align_bytes=64)
+            nc.vector.tensor_copy(
+                out=grouped[:, 0:VECTOR_COLS, :].rearrange("p (c i) j -> p c j i", i=RUN),
+                in_=raw[:, :, 0:VECTOR_COLS].rearrange("p j (c i) -> p c j i", i=RUN),
+            )
+            nc.scalar.copy(
+                out=grouped[:, VECTOR_COLS:UNIT_COLS, :].rearrange("p (c i) j -> p c j i", i=RUN),
+                in_=raw[:, :, VECTOR_COLS:UNIT_COLS].rearrange("p j (c i) -> p c j i", i=RUN),
+            )
+            codes = stage.tile([P, UNIT_COLS], U32, align_bytes=64)
+            scales = stage.tile([P, UNIT_COLS], U8, align_bytes=64)
+            nc.vector.quantize_mx(
+                out=codes[:].bitcast(FP8X4),
+                scales=scales[:],
+                in_=grouped[:].rearrange("p c j -> p (c j)"),
+            )
+
+            y_sb = y_pool.tile([P, M_OUT, A_UNIT, RANK_B], BF16)
+            for half in range(A_UNIT // A_BANK):
+                y_ps = psum_y.tile([P, A_BANK, M_OUT * RANK_B], F32)
+                for q in range(A_BANK):
+                    cols = slice((A_BANK * half + q) * T, (A_BANK * half + q + 1) * T)
+                    nc.tensor.matmul_mx(
+                        out=y_ps[:, q, :],
+                        lhsT=codes[:, cols].bitcast(FP8X4),
+                        lhsT_scale=scales[:, cols],
+                        rhs=w1_codes[:].bitcast(FP8X4),
+                        rhs_scale=w1_scales[:],
+                        start=True,
+                        stop=True,
+                    )
+                nc.scalar.copy(
+                    out=y_sb[:, :, A_BANK * half : A_BANK * (half + 1), :],
+                    in_=y_ps[:].rearrange("p a (m s) -> p m a s", s=RANK_B),
+                )
+
+            if j == 0:
+                t_banks = [
+                    psum_t.tile([P, PACK, 2, T], BF16, name="t_bank%d" % b, tag="t_bank%d" % b)
+                    for b in range(M_OUT // 2)
+                ]
+            for m in range(M_OUT):
+                nc.tensor.transpose(
+                    t_banks[m // 2][:, j, m % 2, :],
+                    y_sb[:, m, :, :].rearrange("p a s -> p (a s)"),
+                    ident[:],
+                )
+
+            if j == PACK - 1:
+                for b in range(M_OUT // 2):
+                    cols = slice(2 * T * b, 2 * T * (b + 1))
+                    d2_grouped = stage.tile([P, 2 * T, PACK], BF16, align_bytes=64)
+                    nc.scalar.copy(
+                        out=d2_grouped[:], in_=t_banks[b][:].rearrange("p j m t -> p (m t) j")
+                    )
+                    nc.vector.quantize_mx(
+                        out=d2_codes[:, g, cols].bitcast(FP8X4),
+                        scales=d2_scales[:, g, cols],
+                        in_=d2_grouped[:].rearrange("p c j -> p (c j)"),
+                    )
+
+        base = keep.tile([P, ROW], F32)
+        nc.vector.tensor_tensor(out=base[:], in0=x_sb[:], in1=mv_sb[:], op=mybir.AluOpType.add)
+        nc.vector.tensor_tensor(out=base[:], in0=base[:], in1=bias_sb[:], op=mybir.AluOpType.add)
+
+        for half in range(2):
+            term_ps = psum_y.tile([P, M_OUT // 2, J_OUT], F32, tag="y_ps")
+            for q in range(M_OUT // 2):
+                m = (M_OUT // 2) * half + q
+                cols = slice(m * T, (m + 1) * T)
+                for g in range(PACK):
+                    nc.tensor.matmul_mx(
+                        out=term_ps[:, q, :],
+                        lhsT=d2_codes[:, g, cols].bitcast(FP8X4),
+                        lhsT_scale=d2_scales[:, g, cols],
+                        rhs=w2_codes[:, g, :].bitcast(FP8X4),
+                        rhs_scale=w2_scales[:, g, :],
+                        start=(g == 0),
+                        stop=(g == PACK - 1),
+                    )
+            cols = slice(half * ROW // 2, (half + 1) * ROW // 2)
+            result = stage.tile([P, ROW // 2], F32)
+            nc.vector.tensor_tensor(
+                out=result[:],
+                in0=base[:, cols],
+                in1=term_ps[:].rearrange("p m o -> p (m o)"),
+                op=mybir.AluOpType.subtract,
+            )
+            nc.sync.dma_start(out=out_rows[:, cols], in_=result[:])

@@ -8,6 +8,8 @@ F32 = mybir.dt.float32
 U32 = mybir.dt.uint32
 U8 = mybir.dt.uint8
 FP8X4 = mybir.dt.float8_e4m3fn_x4
+ADD = mybir.AluOpType.add
+SUBTRACT = mybir.AluOpType.subtract
 
 P = 128
 PACK = 4
@@ -22,8 +24,12 @@ A_UNIT = 8
 UNITS = A // A_UNIT
 UNIT_COLS = A_UNIT * T
 A_BANK = 4
+GROUPS = UNITS // PACK
+M_BANK = 2
+BANKS = M_OUT // M_BANK
 RUN = 4
 VECTOR_COLS = 6 * T
+LAG_BANK = 5
 
 FLOPS = 2 * 512 * 128 * 16384 + 2 * 2048 * 1024 * 128
 
@@ -41,9 +47,10 @@ def tile_ttsolver_pa_t_kernel(tc, d1, g1, g2, x_l, mv, bias, out):
         keep = pools.enter_context(tc.tile_pool(name="keep", bufs=1))
         raw_pool = pools.enter_context(tc.tile_pool(name="raw", bufs=UNITS))
         stage = pools.enter_context(tc.tile_pool(name="stage", bufs=2))
-        y_pool = pools.enter_context(tc.tile_pool(name="y_pool", bufs=3))
-        psum_y = pools.enter_context(tc.psum_pool(name="psum_y", bufs=4))
-        psum_t = pools.enter_context(tc.psum_pool(name="psum_t", bufs=1))
+        psum_y = pools.enter_context(tc.psum_pool(name="psum_y", bufs=3))
+        psum_t = pools.enter_context(tc.psum_pool(name="psum_t", bufs=3))
+        psum_term = pools.enter_context(tc.psum_pool(name="psum_term", bufs=2))
+        pools.enter_context(tc.manual_schedule())
 
         ident = keep.tile([P, P], BF16)
         make_identity(nc, ident[:])
@@ -56,11 +63,11 @@ def tile_ttsolver_pa_t_kernel(tc, d1, g1, g2, x_l, mv, bias, out):
             )
         g2_raw = keep.tile([P, RANK_B, A], BF16)
         nc.sync.dma_start(out=g2_raw[:], in_=g2.rearrange("s o a x -> o s (a x)"))
-        raw_tiles = []
+        raw_of = {}
         for u in range(UNITS):
             raw = raw_pool.tile([P, PACK, UNIT_COLS], BF16)
             nc.sync.dma_start(out=raw[:], in_=d1_rows[:, :, u * UNIT_COLS : (u + 1) * UNIT_COLS])
-            raw_tiles.append(raw)
+            raw_of[u] = raw
         x_sb = keep.tile([P, ROW], BF16)
         nc.sync.dma_start(out=x_sb[:], in_=x_rows)
         mv_sb = keep.tile([P, ROW], BF16)
@@ -81,108 +88,162 @@ def tile_ttsolver_pa_t_kernel(tc, d1, g1, g2, x_l, mv, bias, out):
             in_=w1_grouped[:].rearrange("p m s j -> p (m s j)"),
         )
 
-        g2_sorted = keep.tile([P, A // A_UNIT, A_UNIT, RANK_B], BF16)
+        g2_sorted = keep.tile([P, UNITS, A_UNIT, RANK_B], BF16)
         g2_view = g2_raw[:].rearrange("p s (c a) -> p c a s", a=A_UNIT)
-        nc.vector.tensor_copy(out=g2_sorted[:, 0:8, :, :], in_=g2_view[:, 0:8, :, :])
-        nc.scalar.copy(out=g2_sorted[:, 8:16, :, :], in_=g2_view[:, 8:16, :, :])
-        w2_grouped = keep.tile([P, PACK, J_OUT, PACK], BF16, align_bytes=64)
         for pair in range(2):
-            w_ps = psum_t.tile([P, 2, PACK, J_OUT], BF16, tag="t_bank%d" % pair)
-            for c in range(8):
+            units = slice(8 * pair, 8 * (pair + 1))
+            nc.vector.tensor_copy(out=g2_sorted[:, units, :, :], in_=g2_view[:, units, :, :])
+        w2_grouped = keep.tile([P, GROUPS, J_OUT, PACK], BF16, align_bytes=64)
+        w2_codes = keep.tile([P, GROUPS, J_OUT], U32, align_bytes=64)
+        w2_scales = keep.tile([P, GROUPS, J_OUT], U8, align_bytes=64)
+
+        def transpose_w2(pair):
+            w_ps = psum_t.tile([P, 2, PACK, J_OUT], BF16, tag="t_bank")
+            for c in range(2 * PACK):
                 nc.tensor.transpose(
                     w_ps[:, c // PACK, c % PACK, :],
-                    g2_sorted[:, 8 * pair + c, :, :].rearrange("p a s -> p (a s)"),
+                    g2_sorted[:, 2 * PACK * pair + c, :, :].rearrange("p a s -> p (a s)"),
                     ident[:],
                 )
             nc.scalar.copy(
                 out=w2_grouped[:, 2 * pair : 2 * pair + 2, :, :],
                 in_=w_ps[:].rearrange("p g j o -> p g o j"),
             )
-        w2_codes = keep.tile([P, PACK, J_OUT], U32, align_bytes=64)
-        w2_scales = keep.tile([P, PACK, J_OUT], U8, align_bytes=64)
-        nc.vector.quantize_mx(
-            out=w2_codes[:].rearrange("p g o -> p (g o)").bitcast(FP8X4),
-            scales=w2_scales[:].rearrange("p g o -> p (g o)"),
-            in_=w2_grouped[:].rearrange("p g o j -> p (g o j)"),
-        )
 
-        d2_codes = keep.tile([P, PACK, M_OUT * T], U32, align_bytes=64)
-        d2_scales = keep.tile([P, PACK, M_OUT * T], U8, align_bytes=64)
-        t_banks = []
-        for u in range(UNITS):
-            g, j = divmod(u, PACK)
-            raw = raw_tiles[u]
+        def quantise_w2():
+            nc.vector.quantize_mx(
+                out=w2_codes[:].rearrange("p g o -> p (g o)").bitcast(FP8X4),
+                scales=w2_scales[:].rearrange("p g o -> p (g o)"),
+                in_=w2_grouped[:].rearrange("p g o j -> p (g o j)"),
+            )
+
+        d2_codes = keep.tile([P, GROUPS, M_OUT * T], U32, align_bytes=64)
+        d2_scales = keep.tile([P, GROUPS, M_OUT * T], U8, align_bytes=64)
+        grouped_of = {}
+        codes_of = {}
+        scales_of = {}
+        y_banks_of = {}
+        y_group_of = {}
+        t_bank_of = {}
+        d2_grouped_of = {}
+
+        def regroup_d1(u):
             grouped = stage.tile([P, UNIT_COLS, PACK], BF16, align_bytes=64)
             nc.vector.tensor_copy(
                 out=grouped[:, 0:VECTOR_COLS, :].rearrange("p (c i) j -> p c j i", i=RUN),
-                in_=raw[:, :, 0:VECTOR_COLS].rearrange("p j (c i) -> p c j i", i=RUN),
+                in_=raw_of[u][:, :, 0:VECTOR_COLS].rearrange("p j (c i) -> p c j i", i=RUN),
             )
             nc.scalar.copy(
                 out=grouped[:, VECTOR_COLS:UNIT_COLS, :].rearrange("p (c i) j -> p c j i", i=RUN),
-                in_=raw[:, :, VECTOR_COLS:UNIT_COLS].rearrange("p j (c i) -> p c j i", i=RUN),
+                in_=raw_of[u][:, :, VECTOR_COLS:UNIT_COLS].rearrange("p j (c i) -> p c j i", i=RUN),
             )
+            grouped_of[u] = grouped
+
+        def quantise_d1(u):
             codes = stage.tile([P, UNIT_COLS], U32, align_bytes=64)
             scales = stage.tile([P, UNIT_COLS], U8, align_bytes=64)
             nc.vector.quantize_mx(
                 out=codes[:].bitcast(FP8X4),
                 scales=scales[:],
-                in_=grouped[:].rearrange("p c j -> p (c j)"),
+                in_=grouped_of[u][:].rearrange("p c j -> p (c j)"),
             )
+            codes_of[u] = codes
+            scales_of[u] = scales
 
-            y_sb = y_pool.tile([P, M_OUT, A_UNIT, RANK_B], BF16)
+        def second_core(u):
+            y_banks_of[u] = []
             for half in range(A_UNIT // A_BANK):
                 y_ps = psum_y.tile([P, A_BANK, M_OUT * RANK_B], F32)
                 for q in range(A_BANK):
                     cols = slice((A_BANK * half + q) * T, (A_BANK * half + q + 1) * T)
                     nc.tensor.matmul_mx(
                         out=y_ps[:, q, :],
-                        lhsT=codes[:, cols].bitcast(FP8X4),
-                        lhsT_scale=scales[:, cols],
+                        lhsT=codes_of[u][:, cols].bitcast(FP8X4),
+                        lhsT_scale=scales_of[u][:, cols],
                         rhs=w1_codes[:].bitcast(FP8X4),
                         rhs_scale=w1_scales[:],
                         start=True,
                         stop=True,
                     )
-                nc.scalar.copy(
-                    out=y_sb[:, :, A_BANK * half : A_BANK * (half + 1), :],
-                    in_=y_ps[:].rearrange("p a (m s) -> p m a s", s=RANK_B),
-                )
+                y_banks_of[u].append(y_ps)
 
+        def round_d2(u):
+            g, j = divmod(u, PACK)
             if j == 0:
-                t_banks = [
-                    psum_t.tile([P, PACK, 2, T], BF16, name="t_bank%d" % b, tag="t_bank%d" % b)
-                    for b in range(M_OUT // 2)
-                ]
-            for m in range(M_OUT):
-                nc.tensor.transpose(
-                    t_banks[m // 2][:, j, m % 2, :],
-                    y_sb[:, m, :, :].rearrange("p a s -> p (a s)"),
-                    ident[:],
+                y_group = stage.tile([P, PACK, M_OUT, A_UNIT, RANK_B], BF16)
+                y_group_of[g] = y_group
+            for half in range(A_UNIT // A_BANK):
+                nc.scalar.copy(
+                    out=y_group_of[g][:, j, :, A_BANK * half : A_BANK * (half + 1), :],
+                    in_=y_banks_of[u][half][:].rearrange("p a (m s) -> p m a s", s=RANK_B),
                 )
 
-            if j == PACK - 1:
-                for b in range(M_OUT // 2):
-                    cols = slice(2 * T * b, 2 * T * (b + 1))
-                    d2_grouped = stage.tile([P, 2 * T, PACK], BF16, align_bytes=64)
-                    nc.scalar.copy(
-                        out=d2_grouped[:], in_=t_banks[b][:].rearrange("p j m t -> p (m t) j")
+        def transpose_bank(k):
+            g, b = divmod(k, BANKS)
+            t_bank = psum_t.tile([P, PACK, M_BANK, T], BF16)
+            for j in range(PACK):
+                for q in range(M_BANK):
+                    nc.tensor.transpose(
+                        t_bank[:, j, q, :],
+                        y_group_of[g][:, j, M_BANK * b + q, :, :].rearrange("p a s -> p (a s)"),
+                        ident[:],
                     )
-                    nc.vector.quantize_mx(
-                        out=d2_codes[:, g, cols].bitcast(FP8X4),
-                        scales=d2_scales[:, g, cols],
-                        in_=d2_grouped[:].rearrange("p c j -> p (c j)"),
-                    )
+            t_bank_of[k] = t_bank
+
+        def regroup_d2(k, copy):
+            d2_grouped = stage.tile([P, M_BANK * T, PACK], BF16, align_bytes=64, bufs=BANKS)
+            copy(out=d2_grouped[:], in_=t_bank_of[k][:].rearrange("p j m t -> p (m t) j"))
+            d2_grouped_of[k] = d2_grouped
+
+        def quantise_d2(k):
+            g, b = divmod(k, BANKS)
+            cols = slice(M_BANK * T * b, M_BANK * T * (b + 1))
+            nc.vector.quantize_mx(
+                out=d2_codes[:, g, cols].bitcast(FP8X4),
+                scales=d2_scales[:, g, cols],
+                in_=d2_grouped_of[k][:].rearrange("p c j -> p (c j)"),
+            )
+
+        for i in range(UNITS + 1):
+            k = i - LAG_BANK
+            if i >= 1:
+                quantise_d1(i - 1)
+            if i < UNITS:
+                regroup_d1(i)
+            if i < 2:
+                transpose_w2(i)
+            if i == 2:
+                quantise_w2()
+            if k >= 0:
+                transpose_bank(k)
+            if i >= 1:
+                second_core(i - 1)
+            if k >= 0:
+                regroup_d2(k, nc.scalar.copy)
+            if i >= 1:
+                round_d2(i - 1)
+            if k >= 0:
+                quantise_d2(k)
 
         base = keep.tile([P, ROW], F32)
-        nc.vector.tensor_tensor(out=base[:], in0=x_sb[:], in1=mv_sb[:], op=mybir.AluOpType.add)
-        nc.vector.tensor_tensor(out=base[:], in0=base[:], in1=bias_sb[:], op=mybir.AluOpType.add)
+        nc.vector.tensor_tensor(out=base[:], in0=x_sb[:], in1=mv_sb[:], op=ADD)
+        nc.vector.tensor_tensor(out=base[:], in0=base[:], in1=bias_sb[:], op=ADD)
+
+        first = (GROUPS - 1) * BANKS
+        for b in range(BANKS):
+            transpose_bank(first + b)
+        for b in range(0, BANKS, 2):
+            regroup_d2(first + b, nc.scalar.copy)
+            regroup_d2(first + b + 1, nc.vector.tensor_copy)
+            quantise_d2(first + b)
+            quantise_d2(first + b + 1)
 
         for half in range(2):
-            term_ps = psum_y.tile([P, M_OUT // 2, J_OUT], F32, tag="y_ps")
+            term_ps = psum_term.tile([P, M_OUT // 2, J_OUT], F32)
             for q in range(M_OUT // 2):
                 m = (M_OUT // 2) * half + q
                 cols = slice(m * T, (m + 1) * T)
-                for g in range(PACK):
+                for g in range(GROUPS):
                     nc.tensor.matmul_mx(
                         out=term_ps[:, q, :],
                         lhsT=d2_codes[:, g, cols].bitcast(FP8X4),
@@ -190,7 +251,7 @@ def tile_ttsolver_pa_t_kernel(tc, d1, g1, g2, x_l, mv, bias, out):
                         rhs=w2_codes[:, g, :].bitcast(FP8X4),
                         rhs_scale=w2_scales[:, g, :],
                         start=(g == 0),
-                        stop=(g == PACK - 1),
+                        stop=(g == GROUPS - 1),
                     )
             cols = slice(half * ROW // 2, (half + 1) * ROW // 2)
             result = stage.tile([P, ROW // 2], F32)
@@ -198,6 +259,6 @@ def tile_ttsolver_pa_t_kernel(tc, d1, g1, g2, x_l, mv, bias, out):
                 out=result[:],
                 in0=base[:, cols],
                 in1=term_ps[:].rearrange("p m o -> p (m o)"),
-                op=mybir.AluOpType.subtract,
+                op=SUBTRACT,
             )
             nc.sync.dma_start(out=out_rows[:, cols], in_=result[:])

@@ -23,12 +23,15 @@ ROW = M_OUT * J_OUT
 A_UNIT = 8
 UNITS = A // A_UNIT
 UNIT_COLS = A_UNIT * T
+PAIR = 2
 A_BANK = 4
+POSITIONS = A_BANK * T
+T_HALF = T // PAIR
 GROUPS = UNITS // PACK
 M_BANK = 2
 BANKS = M_OUT // M_BANK
 RUN = 4
-VECTOR_COLS = 6 * T
+VECTOR_POSITIONS = 352
 LAG_BANK = 5
 
 FLOPS = 2 * 512 * 128 * 16384 + 2 * 2048 * 1024 * 128
@@ -65,8 +68,10 @@ def tile_ttsolver_pa_t_kernel(tc, d1, g1, g2, x_l, mv, bias, out):
         nc.sync.dma_start(out=g2_raw[:], in_=g2.rearrange("s o a x -> o s (a x)"))
         raw_of = {}
         for u in range(UNITS):
-            raw = raw_pool.tile([P, PACK, UNIT_COLS], BF16)
-            nc.sync.dma_start(out=raw[:], in_=d1_rows[:, :, u * UNIT_COLS : (u + 1) * UNIT_COLS])
+            raw = raw_pool.tile([P, PAIR, PACK, POSITIONS], BF16)
+            for e in range(PAIR):
+                start = (16 * (u // 2) + 8 * e + A_BANK * (u % 2)) * T
+                nc.sync.dma_start(out=raw[:, e, :, :], in_=d1_rows[:, :, start : start + POSITIONS])
             raw_of[u] = raw
         x_sb = keep.tile([P, ROW], BF16)
         nc.sync.dma_start(out=x_sb[:], in_=x_rows)
@@ -128,15 +133,16 @@ def tile_ttsolver_pa_t_kernel(tc, d1, g1, g2, x_l, mv, bias, out):
         d2_grouped_of = {}
 
         def regroup_d1(u):
-            grouped = stage.tile([P, UNIT_COLS, PACK], BF16, align_bytes=64)
-            nc.vector.tensor_copy(
-                out=grouped[:, 0:VECTOR_COLS, :].rearrange("p (c i) j -> p c j i", i=RUN),
-                in_=raw_of[u][:, :, 0:VECTOR_COLS].rearrange("p j (c i) -> p c j i", i=RUN),
-            )
-            nc.scalar.copy(
-                out=grouped[:, VECTOR_COLS:UNIT_COLS, :].rearrange("p (c i) j -> p c j i", i=RUN),
-                in_=raw_of[u][:, :, VECTOR_COLS:UNIT_COLS].rearrange("p j (c i) -> p c j i", i=RUN),
-            )
+            grouped = stage.tile([P, POSITIONS, PAIR * PACK], BF16, align_bytes=64)
+
+            def interleave(copy, cols):
+                copy(
+                    out=grouped[:, cols, :].rearrange("p (c i) x -> p c x i", i=RUN),
+                    in_=raw_of[u][:, :, :, cols].rearrange("p e j (c i) -> p c (e j) i", i=RUN),
+                )
+
+            interleave(nc.vector.tensor_copy, slice(0, VECTOR_POSITIONS))
+            interleave(nc.scalar.copy, slice(VECTOR_POSITIONS, POSITIONS))
             grouped_of[u] = grouped
 
         def quantise_d1(u):
@@ -145,17 +151,17 @@ def tile_ttsolver_pa_t_kernel(tc, d1, g1, g2, x_l, mv, bias, out):
             nc.vector.quantize_mx(
                 out=codes[:].bitcast(FP8X4),
                 scales=scales[:],
-                in_=grouped_of[u][:].rearrange("p c j -> p (c j)"),
+                in_=grouped_of[u][:].rearrange("p c x -> p (c x)"),
             )
             codes_of[u] = codes
             scales_of[u] = scales
 
         def second_core(u):
             y_banks_of[u] = []
-            for half in range(A_UNIT // A_BANK):
+            for half in range(PAIR):
                 y_ps = psum_y.tile([P, A_BANK, M_OUT * RANK_B], F32)
                 for q in range(A_BANK):
-                    cols = slice((A_BANK * half + q) * T, (A_BANK * half + q + 1) * T)
+                    cols = slice((PAIR * q + half) * P, (PAIR * q + half + 1) * P)
                     nc.tensor.matmul_mx(
                         out=y_ps[:, q, :],
                         lhsT=codes_of[u][:, cols].bitcast(FP8X4),
@@ -168,31 +174,34 @@ def tile_ttsolver_pa_t_kernel(tc, d1, g1, g2, x_l, mv, bias, out):
                 y_banks_of[u].append(y_ps)
 
         def round_d2(u):
-            g, j = divmod(u, PACK)
-            if j == 0:
-                y_group = stage.tile([P, PACK, M_OUT, A_UNIT, RANK_B], BF16)
+            g = u // PACK
+            v = (u // 2) % 2
+            quad = slice(A_BANK * (u % 2), A_BANK * (u % 2 + 1))
+            if u % PACK == 0:
+                y_group = stage.tile([P, 2, PAIR, M_OUT, A_UNIT, RANK_B], BF16)
                 y_group_of[g] = y_group
-            for half in range(A_UNIT // A_BANK):
+            for half in range(PAIR):
                 nc.scalar.copy(
-                    out=y_group_of[g][:, j, :, A_BANK * half : A_BANK * (half + 1), :],
+                    out=y_group_of[g][:, v, half, :, quad, :],
                     in_=y_banks_of[u][half][:].rearrange("p a (m s) -> p m a s", s=RANK_B),
                 )
 
         def transpose_bank(k):
             g, b = divmod(k, BANKS)
-            t_bank = psum_t.tile([P, PACK, M_BANK, T], BF16)
-            for j in range(PACK):
-                for q in range(M_BANK):
-                    nc.tensor.transpose(
-                        t_bank[:, j, q, :],
-                        y_group_of[g][:, j, M_BANK * b + q, :, :].rearrange("p a s -> p (a s)"),
-                        ident[:],
-                    )
+            t_bank = psum_t.tile([P, M_BANK, PAIR, T_HALF, 2, PAIR], BF16)
+            for q in range(M_BANK):
+                for half in range(PAIR):
+                    for v in range(2):
+                        nc.tensor.transpose(
+                            t_bank[:, q, half, :, v, :],
+                            y_group_of[g][:, v, half, M_BANK * b + q, :, :].rearrange("p a s -> p (a s)"),
+                            ident[:],
+                        )
             t_bank_of[k] = t_bank
 
         def regroup_d2(k, copy):
             d2_grouped = stage.tile([P, M_BANK * T, PACK], BF16, align_bytes=64, bufs=BANKS)
-            copy(out=d2_grouped[:], in_=t_bank_of[k][:].rearrange("p j m t -> p (m t) j"))
+            copy(out=d2_grouped[:], in_=t_bank_of[k][:].rearrange("p m h t v e -> p (m h t) (v e)"))
             d2_grouped_of[k] = d2_grouped
 
         def quantise_d2(k):

@@ -31,7 +31,7 @@ GROUPS = UNITS // PACK
 M_BANK = 2
 BANKS = M_OUT // M_BANK
 RUN = 4
-VECTOR_POSITIONS = 352
+VECTOR_POSITIONS = 384
 LAG_BANK = 5
 
 FLOPS = 2 * 512 * 128 * 16384 + 2 * 2048 * 1024 * 128
@@ -59,13 +59,7 @@ def tile_ttsolver_pa_t_kernel(tc, d1, g1, g2, x_l, mv, bias, out):
         make_identity(nc, ident[:])
 
         g1_raw = keep.tile([P, M_OUT, PACK * RANK_B], BF16)
-        for h in range(2):
-            nc.sync.dma_start(
-                out=g1_raw[h:P:2, :, :],
-                in_=g1[:, :, PACK * h : PACK * (h + 1), :].rearrange("r m j s -> r m (j s)"),
-            )
         g2_raw = keep.tile([P, RANK_B, A], BF16)
-        nc.sync.dma_start(out=g2_raw[:], in_=g2.rearrange("s o a x -> o s (a x)"))
         raw_of = {}
         for u in range(UNITS):
             raw = raw_pool.tile([P, PAIR, PACK, POSITIONS], BF16)
@@ -73,6 +67,13 @@ def tile_ttsolver_pa_t_kernel(tc, d1, g1, g2, x_l, mv, bias, out):
                 start = (16 * (u // 2) + 8 * e + A_BANK * (u % 2)) * T
                 nc.sync.dma_start(out=raw[:, e, :, :], in_=d1_rows[:, :, start : start + POSITIONS])
             raw_of[u] = raw
+            if u == 0:
+                for h in range(2):
+                    nc.sync.dma_start(
+                        out=g1_raw[h:P:2, :, :],
+                        in_=g1[:, :, PACK * h : PACK * (h + 1), :].rearrange("r m j s -> r m (j s)"),
+                    )
+        nc.sync.dma_start(out=g2_raw[:], in_=g2.rearrange("s o a x -> o s (a x)"))
         x_sb = keep.tile([P, ROW], BF16)
         nc.sync.dma_start(out=x_sb[:], in_=x_rows)
         mv_sb = keep.tile([P, ROW], BF16)
@@ -82,22 +83,28 @@ def tile_ttsolver_pa_t_kernel(tc, d1, g1, g2, x_l, mv, bias, out):
             nc.sync.dma_start(out=bias_sb[16 * b : 16 * (b + 1), :], in_=bias_rows)
 
         w1_grouped = keep.tile([P, M_OUT, RANK_B, PACK], BF16, align_bytes=64)
-        nc.vector.tensor_copy(
-            out=w1_grouped[:], in_=g1_raw[:].rearrange("p m (j s) -> p m s j", j=PACK)
-        )
         w1_codes = keep.tile([P, M_OUT * RANK_B], U32, align_bytes=64)
         w1_scales = keep.tile([P, M_OUT * RANK_B], U8, align_bytes=64)
-        nc.vector.quantize_mx(
-            out=w1_codes[:].bitcast(FP8X4),
-            scales=w1_scales[:],
-            in_=w1_grouped[:].rearrange("p m s j -> p (m s j)"),
-        )
+
+        def regroup_w1():
+            nc.vector.tensor_copy(
+                out=w1_grouped[:], in_=g1_raw[:].rearrange("p m (j s) -> p m s j", j=PACK)
+            )
+
+        def quantise_w1():
+            nc.vector.quantize_mx(
+                out=w1_codes[:].bitcast(FP8X4),
+                scales=w1_scales[:],
+                in_=w1_grouped[:].rearrange("p m s j -> p (m s j)"),
+            )
 
         g2_sorted = keep.tile([P, UNITS, A_UNIT, RANK_B], BF16)
         g2_view = g2_raw[:].rearrange("p s (c a) -> p c a s", a=A_UNIT)
-        for pair in range(2):
+
+        def sort_w2(pair):
             units = slice(8 * pair, 8 * (pair + 1))
             nc.vector.tensor_copy(out=g2_sorted[:, units, :, :], in_=g2_view[:, units, :, :])
+
         w2_grouped = keep.tile([P, GROUPS, J_OUT, PACK], BF16, align_bytes=64)
         w2_codes = keep.tile([P, GROUPS, J_OUT], U32, align_bytes=64)
         w2_scales = keep.tile([P, GROUPS, J_OUT], U8, align_bytes=64)
@@ -215,13 +222,19 @@ def tile_ttsolver_pa_t_kernel(tc, d1, g1, g2, x_l, mv, bias, out):
 
         for i in range(UNITS + 1):
             k = i - LAG_BANK
+            if i == 1:
+                regroup_w1()
             if i >= 1:
                 quantise_d1(i - 1)
+            if i == 1:
+                quantise_w1()
             if i < UNITS:
                 regroup_d1(i)
-            if i < 2:
-                transpose_w2(i)
-            if i == 2:
+            if 11 <= i < 13:
+                sort_w2(i - 11)
+            if 12 <= i < 14:
+                transpose_w2(i - 12)
+            if i == 14:
                 quantise_w2()
             if k >= 0:
                 transpose_bank(k)

@@ -25,13 +25,13 @@ UNITS = A // A_UNIT
 UNIT_COLS = A_UNIT * T
 PAIR = 2
 A_BANK = 4
+Q_BANK = A_BANK // PAIR
 POSITIONS = A_BANK * T
-T_HALF = T // PAIR
 GROUPS = UNITS // PACK
 M_BANK = 2
 BANKS = M_OUT // M_BANK
 RUN = 4
-VECTOR_POSITIONS = 384
+VECTOR_POSITIONS = 336
 LAG_BANK = 5
 
 FLOPS = 2 * 512 * 128 * 16384 + 2 * 2048 * 1024 * 128
@@ -57,6 +57,8 @@ def tile_ttsolver_pa_t_kernel(tc, d1, g1, g2, x_l, mv, bias, out):
 
         ident = keep.tile([P, P], BF16)
         make_identity(nc, ident[:])
+        ident_words = keep.tile([P, P], F32)
+        make_identity(nc, ident_words[:])
 
         g1_raw = keep.tile([P, M_OUT, PACK * RANK_B], BF16)
         g2_raw = keep.tile([P, RANK_B, A], BF16)
@@ -140,12 +142,12 @@ def tile_ttsolver_pa_t_kernel(tc, d1, g1, g2, x_l, mv, bias, out):
         d2_grouped_of = {}
 
         def regroup_d1(u):
-            grouped = stage.tile([P, POSITIONS, PAIR * PACK], BF16, align_bytes=64)
+            grouped = stage.tile([P, PAIR, POSITIONS, PACK], BF16, align_bytes=64)
 
             def interleave(copy, cols):
                 copy(
-                    out=grouped[:, cols, :].rearrange("p (c i) x -> p c x i", i=RUN),
-                    in_=raw_of[u][:, :, :, cols].rearrange("p e j (c i) -> p c (e j) i", i=RUN),
+                    out=grouped[:, :, cols, :].rearrange("p e (c i) j -> p e c j i", i=RUN),
+                    in_=raw_of[u][:, :, :, cols].rearrange("p e j (c i) -> p e c j i", i=RUN),
                 )
 
             interleave(nc.vector.tensor_copy, slice(0, VECTOR_POSITIONS))
@@ -158,57 +160,59 @@ def tile_ttsolver_pa_t_kernel(tc, d1, g1, g2, x_l, mv, bias, out):
             nc.vector.quantize_mx(
                 out=codes[:].bitcast(FP8X4),
                 scales=scales[:],
-                in_=grouped_of[u][:].rearrange("p c x -> p (c x)"),
+                in_=grouped_of[u][:].rearrange("p e c j -> p (e c j)"),
             )
             codes_of[u] = codes
             scales_of[u] = scales
 
         def second_core(u):
             y_banks_of[u] = []
-            for half in range(PAIR):
-                y_ps = psum_y.tile([P, A_BANK, M_OUT * RANK_B], F32)
-                for q in range(A_BANK):
-                    cols = slice((PAIR * q + half) * P, (PAIR * q + half + 1) * P)
-                    nc.tensor.matmul_mx(
-                        out=y_ps[:, q, :],
-                        lhsT=codes_of[u][:, cols].bitcast(FP8X4),
-                        lhsT_scale=scales_of[u][:, cols],
-                        rhs=w1_codes[:].bitcast(FP8X4),
-                        rhs_scale=w1_scales[:],
-                        start=True,
-                        stop=True,
-                    )
+            for first in range(0, A_BANK, Q_BANK):
+                y_ps = psum_y.tile([P, PAIR, Q_BANK, M_OUT * RANK_B], F32)
+                for e in range(PAIR):
+                    for q in range(Q_BANK):
+                        start = (A_BANK * e + first + q) * T
+                        cols = slice(start, start + T)
+                        nc.tensor.matmul_mx(
+                            out=y_ps[:, e, q, :],
+                            lhsT=codes_of[u][:, cols].bitcast(FP8X4),
+                            lhsT_scale=scales_of[u][:, cols],
+                            rhs=w1_codes[:].bitcast(FP8X4),
+                            rhs_scale=w1_scales[:],
+                            start=True,
+                            stop=True,
+                        )
                 y_banks_of[u].append(y_ps)
 
         def round_d2(u):
             g = u // PACK
             v = (u // 2) % 2
-            quad = slice(A_BANK * (u % 2), A_BANK * (u % 2 + 1))
             if u % PACK == 0:
-                y_group = stage.tile([P, 2, PAIR, M_OUT, A_UNIT, RANK_B], BF16)
+                y_group = stage.tile([P, 2, M_OUT, A_UNIT, RANK_B, PAIR], BF16)
                 y_group_of[g] = y_group
-            for half in range(PAIR):
+            for b in range(PAIR):
+                first = A_BANK * (u % 2) + Q_BANK * b
                 nc.scalar.copy(
-                    out=y_group_of[g][:, v, half, :, quad, :],
-                    in_=y_banks_of[u][half][:].rearrange("p a (m s) -> p m a s", s=RANK_B),
+                    out=y_group_of[g][:, v, :, first : first + Q_BANK, :, :],
+                    in_=y_banks_of[u][b][:].rearrange("p e q (m s) -> p m q s e", s=RANK_B),
                 )
 
         def transpose_bank(k):
             g, b = divmod(k, BANKS)
-            t_bank = psum_t.tile([P, M_BANK, PAIR, T_HALF, 2, PAIR], BF16)
+            t_bank = psum_t.tile([P, M_BANK, 2, T], F32)
             for q in range(M_BANK):
-                for half in range(PAIR):
-                    for v in range(2):
-                        nc.tensor.transpose(
-                            t_bank[:, q, half, :, v, :],
-                            y_group_of[g][:, v, half, M_BANK * b + q, :, :].rearrange("p a s -> p (a s)"),
-                            ident[:],
-                        )
+                for v in range(2):
+                    y_words = y_group_of[g][:, v, M_BANK * b + q, :, :, :].rearrange("p a s e -> p (a s e)")
+                    nc.tensor.transpose(t_bank[:, q, v, :], y_words.bitcast(F32), ident_words[:])
             t_bank_of[k] = t_bank
 
         def regroup_d2(k, copy):
             d2_grouped = stage.tile([P, M_BANK * T, PACK], BF16, align_bytes=64, bufs=BANKS)
-            copy(out=d2_grouped[:], in_=t_bank_of[k][:].rearrange("p m h t v e -> p (m h t) (v e)"))
+            words = d2_grouped[:].rearrange("p c j -> p (c j)").bitcast(F32)
+            copy(
+                out=words.rearrange("p (q t v) -> p q t v", q=M_BANK, v=2),
+                in_=t_bank_of[k][:].rearrange("p q v t -> p q t v"),
+            )
             d2_grouped_of[k] = d2_grouped
 
         def quantise_d2(k):

@@ -20,18 +20,19 @@ RANK_B = 16
 J_OUT = 128
 ROW = M_OUT * J_OUT
 
+PAIR = 2
 A_UNIT = 8
 UNITS = A // A_UNIT
 UNIT_COLS = A_UNIT * T
-PAIR = 2
 A_BANK = 4
 Q_BANK = A_BANK // PAIR
-POSITIONS = A_BANK * T
+A_LO = 8
 GROUPS = UNITS // PACK
 M_BANK = 2
 BANKS = M_OUT // M_BANK
 RUN = 4
-VECTOR_POSITIONS = 336
+VECTOR_COLS = 640
+TENSOR_COLS = 112
 LAG_BANK = 5
 
 FLOPS = 2 * 512 * 128 * 16384 + 2 * 2048 * 1024 * 128
@@ -48,26 +49,27 @@ def tile_ttsolver_pa_t_kernel(tc, d1, g1, g2, x_l, mv, bias, out):
 
     with ExitStack() as pools:
         keep = pools.enter_context(tc.tile_pool(name="keep", bufs=1))
-        raw_pool = pools.enter_context(tc.tile_pool(name="raw", bufs=UNITS))
+        raw_pool = pools.enter_context(tc.tile_pool(name="raw", bufs=12))
         stage = pools.enter_context(tc.tile_pool(name="stage", bufs=2))
         psum_y = pools.enter_context(tc.psum_pool(name="psum_y", bufs=3))
         psum_t = pools.enter_context(tc.psum_pool(name="psum_t", bufs=3))
-        psum_term = pools.enter_context(tc.psum_pool(name="psum_term", bufs=2))
+        psum_d1 = pools.enter_context(tc.psum_pool(name="psum_d1", bufs=2))
         pools.enter_context(tc.manual_schedule())
 
-        ident = keep.tile([P, P], BF16)
+        ident = keep.tile([P, P], F32)
         make_identity(nc, ident[:])
-        ident_words = keep.tile([P, P], F32)
-        make_identity(nc, ident_words[:])
+        ident_bf16 = keep.tile([P, P], BF16)
+        make_identity(nc, ident_bf16[:])
 
         g1_raw = keep.tile([P, M_OUT, PACK * RANK_B], BF16)
         g2_raw = keep.tile([P, RANK_B, A], BF16)
         raw_of = {}
         for u in range(UNITS):
-            raw = raw_pool.tile([P, PAIR, PACK, POSITIONS], BF16)
-            for e in range(PAIR):
-                start = (16 * (u // 2) + 8 * e + A_BANK * (u % 2)) * T
-                nc.sync.dma_start(out=raw[:, e, :, :], in_=d1_rows[:, :, start : start + POSITIONS])
+            raw = raw_pool.tile([P, PACK, UNIT_COLS], BF16)
+            for half in range(2):
+                cols = slice(half * UNIT_COLS // 2, (half + 1) * UNIT_COLS // 2)
+                start = u * UNIT_COLS + half * UNIT_COLS // 2
+                nc.sync.dma_start(out=raw[:, :, cols], in_=d1_rows[:, :, start : start + UNIT_COLS // 2])
             raw_of[u] = raw
             if u == 0:
                 for h in range(2):
@@ -100,28 +102,29 @@ def tile_ttsolver_pa_t_kernel(tc, d1, g1, g2, x_l, mv, bias, out):
                 in_=w1_grouped[:].rearrange("p m s j -> p (m s j)"),
             )
 
-        g2_sorted = keep.tile([P, UNITS, A_UNIT, RANK_B], BF16)
-        g2_view = g2_raw[:].rearrange("p s (c a) -> p c a s", a=A_UNIT)
-
-        def sort_w2(pair):
-            units = slice(8 * pair, 8 * (pair + 1))
-            nc.vector.tensor_copy(out=g2_sorted[:, units, :, :], in_=g2_view[:, units, :, :])
-
+        g2_sorted = keep.tile([P, 2 * GROUPS, A_LO, RANK_B], F32)
         w2_grouped = keep.tile([P, GROUPS, J_OUT, PACK], BF16, align_bytes=64)
         w2_codes = keep.tile([P, GROUPS, J_OUT], U32, align_bytes=64)
         w2_scales = keep.tile([P, GROUPS, J_OUT], U8, align_bytes=64)
 
-        def transpose_w2(pair):
-            w_ps = psum_t.tile([P, 2, PACK, J_OUT], BF16, tag="t_bank")
-            for c in range(2 * PACK):
+        def sort_w2():
+            words = g2_raw[:].rearrange("p s a -> p (s a)").bitcast(F32)
+            nc.vector.tensor_copy(
+                out=g2_sorted[:], in_=words.rearrange("p (s c a) -> p c a s", s=RANK_B, a=A_LO)
+            )
+
+        def transpose_w2(h):
+            w_ps = psum_t.tile([P, 2, 2, J_OUT], F32, tag="t_bank")
+            for c in range(4):
                 nc.tensor.transpose(
-                    w_ps[:, c // PACK, c % PACK, :],
-                    g2_sorted[:, 2 * PACK * pair + c, :, :].rearrange("p a s -> p (a s)"),
+                    w_ps[:, c // 2, c % 2, :],
+                    g2_sorted[:, 4 * h + c, :, :].rearrange("p a s -> p (a s)"),
                     ident[:],
                 )
+            words = w2_grouped[:, 2 * h : 2 * h + 2, :, :].rearrange("p g o j -> p (g o j)").bitcast(F32)
             nc.scalar.copy(
-                out=w2_grouped[:, 2 * pair : 2 * pair + 2, :, :],
-                in_=w_ps[:].rearrange("p g j o -> p g o j"),
+                out=words.rearrange("p (g o v) -> p g o v", g=2, v=2),
+                in_=w_ps[:].rearrange("p g v o -> p g o v"),
             )
 
         def quantise_w2():
@@ -141,60 +144,72 @@ def tile_ttsolver_pa_t_kernel(tc, d1, g1, g2, x_l, mv, bias, out):
         t_bank_of = {}
         d2_grouped_of = {}
 
+        ordered_of = {}
+
+        def order_d1(u):
+            ordered = psum_d1.tile([P, TENSOR_COLS, PACK], BF16)
+            nc.tensor.matmul(
+                ordered[:],
+                lhsT=ident_bf16[:],
+                rhs=raw_of[u][:, :, UNIT_COLS - TENSOR_COLS :].rearrange("p j c -> p c j"),
+                start=True,
+                stop=True,
+            )
+            ordered_of[u] = ordered
+
         def regroup_d1(u):
-            grouped = stage.tile([P, PAIR, POSITIONS, PACK], BF16, align_bytes=64)
+            grouped = stage.tile([P, UNIT_COLS, PACK], BF16, align_bytes=64, bufs=3)
 
             def interleave(copy, cols):
                 copy(
-                    out=grouped[:, :, cols, :].rearrange("p e (c i) j -> p e c j i", i=RUN),
-                    in_=raw_of[u][:, :, :, cols].rearrange("p e j (c i) -> p e c j i", i=RUN),
+                    out=grouped[:, cols, :].rearrange("p (c i) j -> p c j i", i=RUN),
+                    in_=raw_of[u][:, :, cols].rearrange("p j (c i) -> p c j i", i=RUN),
                 )
 
-            interleave(nc.vector.tensor_copy, slice(0, VECTOR_POSITIONS))
-            interleave(nc.scalar.copy, slice(VECTOR_POSITIONS, POSITIONS))
+            interleave(nc.vector.tensor_copy, slice(0, VECTOR_COLS))
+            interleave(nc.scalar.copy, slice(VECTOR_COLS, UNIT_COLS - TENSOR_COLS))
+            nc.scalar.copy(out=grouped[:, UNIT_COLS - TENSOR_COLS :, :], in_=ordered_of[u][:])
             grouped_of[u] = grouped
 
         def quantise_d1(u):
-            codes = stage.tile([P, UNIT_COLS], U32, align_bytes=64)
-            scales = stage.tile([P, UNIT_COLS], U8, align_bytes=64)
+            codes = stage.tile([P, UNIT_COLS], U32, align_bytes=64, bufs=4)
+            scales = stage.tile([P, UNIT_COLS], U8, align_bytes=64, bufs=4)
             nc.vector.quantize_mx(
                 out=codes[:].bitcast(FP8X4),
                 scales=scales[:],
-                in_=grouped_of[u][:].rearrange("p e c j -> p (e c j)"),
+                in_=grouped_of[u][:].rearrange("p c j -> p (c j)"),
             )
             codes_of[u] = codes
             scales_of[u] = scales
 
         def second_core(u):
             y_banks_of[u] = []
-            for first in range(0, A_BANK, Q_BANK):
-                y_ps = psum_y.tile([P, PAIR, Q_BANK, M_OUT * RANK_B], F32)
-                for e in range(PAIR):
-                    for q in range(Q_BANK):
-                        start = (A_BANK * e + first + q) * T
-                        cols = slice(start, start + T)
-                        nc.tensor.matmul_mx(
-                            out=y_ps[:, e, q, :],
-                            lhsT=codes_of[u][:, cols].bitcast(FP8X4),
-                            lhsT_scale=scales_of[u][:, cols],
-                            rhs=w1_codes[:].bitcast(FP8X4),
-                            rhs_scale=w1_scales[:],
-                            start=True,
-                            stop=True,
-                        )
+            for b in range(A_UNIT // A_BANK):
+                y_ps = psum_y.tile([P, A_BANK, M_OUT * RANK_B], F32)
+                for i in range(A_BANK):
+                    cols = slice((A_BANK * b + i) * T, (A_BANK * b + i + 1) * T)
+                    nc.tensor.matmul_mx(
+                        out=y_ps[:, i, :],
+                        lhsT=codes_of[u][:, cols].bitcast(FP8X4),
+                        lhsT_scale=scales_of[u][:, cols],
+                        rhs=w1_codes[:].bitcast(FP8X4),
+                        rhs_scale=w1_scales[:],
+                        start=True,
+                        stop=True,
+                    )
                 y_banks_of[u].append(y_ps)
 
         def round_d2(u):
             g = u // PACK
             v = (u // 2) % 2
             if u % PACK == 0:
-                y_group = stage.tile([P, 2, M_OUT, A_UNIT, RANK_B, PAIR], BF16)
+                y_group = stage.tile([P, 2, M_OUT, A_LO, RANK_B, PAIR], BF16)
                 y_group_of[g] = y_group
-            for b in range(PAIR):
-                first = A_BANK * (u % 2) + Q_BANK * b
+            for b in range(A_UNIT // A_BANK):
+                first = A_UNIT // PAIR * (u % 2) + Q_BANK * b
                 nc.scalar.copy(
                     out=y_group_of[g][:, v, :, first : first + Q_BANK, :, :],
-                    in_=y_banks_of[u][b][:].rearrange("p e q (m s) -> p m q s e", s=RANK_B),
+                    in_=y_banks_of[u][b][:].rearrange("p (q e) (m s) -> p m q s e", e=PAIR, s=RANK_B),
                 )
 
         def transpose_bank(k):
@@ -203,29 +218,32 @@ def tile_ttsolver_pa_t_kernel(tc, d1, g1, g2, x_l, mv, bias, out):
             for q in range(M_BANK):
                 for v in range(2):
                     y_words = y_group_of[g][:, v, M_BANK * b + q, :, :, :].rearrange("p a s e -> p (a s e)")
-                    nc.tensor.transpose(t_bank[:, q, v, :], y_words.bitcast(F32), ident_words[:])
+                    nc.tensor.transpose(t_bank[:, q, v, :], y_words.bitcast(F32), ident[:])
             t_bank_of[k] = t_bank
 
         def regroup_d2(k, copy):
-            d2_grouped = stage.tile([P, M_BANK * T, PACK], BF16, align_bytes=64, bufs=BANKS)
-            words = d2_grouped[:].rearrange("p c j -> p (c j)").bitcast(F32)
+            if k % 2 == 0:
+                d2_grouped = stage.tile([P, 2, M_BANK * T, PACK], BF16, align_bytes=64, bufs=3)
+                d2_grouped_of[k // 2] = d2_grouped
+            words = d2_grouped_of[k // 2][:, k % 2, :, :].rearrange("p c j -> p (c j)").bitcast(F32)
             copy(
                 out=words.rearrange("p (q t v) -> p q t v", q=M_BANK, v=2),
                 in_=t_bank_of[k][:].rearrange("p q v t -> p q t v"),
             )
-            d2_grouped_of[k] = d2_grouped
 
-        def quantise_d2(k):
-            g, b = divmod(k, BANKS)
-            cols = slice(M_BANK * T * b, M_BANK * T * (b + 1))
+        def quantise_d2(pair):
+            g, b = divmod(pair, BANKS // 2)
+            cols = slice(2 * M_BANK * T * b, 2 * M_BANK * T * (b + 1))
             nc.vector.quantize_mx(
                 out=d2_codes[:, g, cols].bitcast(FP8X4),
                 scales=d2_scales[:, g, cols],
-                in_=d2_grouped_of[k][:].rearrange("p c j -> p (c j)"),
+                in_=d2_grouped_of[pair][:].rearrange("p b c j -> p (b c j)"),
             )
 
         for i in range(UNITS + 1):
             k = i - LAG_BANK
+            if i == 0:
+                order_d1(0)
             if i == 1:
                 regroup_w1()
             if i >= 1:
@@ -234,8 +252,8 @@ def tile_ttsolver_pa_t_kernel(tc, d1, g1, g2, x_l, mv, bias, out):
                 quantise_w1()
             if i < UNITS:
                 regroup_d1(i)
-            if 11 <= i < 13:
-                sort_w2(i - 11)
+            if i == 11:
+                sort_w2()
             if 12 <= i < 14:
                 transpose_w2(i - 12)
             if i == 14:
@@ -244,12 +262,14 @@ def tile_ttsolver_pa_t_kernel(tc, d1, g1, g2, x_l, mv, bias, out):
                 transpose_bank(k)
             if i >= 1:
                 second_core(i - 1)
+            if i + 1 < UNITS:
+                order_d1(i + 1)
             if k >= 0:
                 regroup_d2(k, nc.scalar.copy)
             if i >= 1:
                 round_d2(i - 1)
-            if k >= 0:
-                quantise_d2(k)
+            if k >= 0 and k % 2 == 1:
+                quantise_d2(k // 2)
 
         base = keep.tile([P, ROW], F32)
         nc.vector.tensor_tensor(out=base[:], in0=x_sb[:], in1=mv_sb[:], op=ADD)
@@ -261,11 +281,10 @@ def tile_ttsolver_pa_t_kernel(tc, d1, g1, g2, x_l, mv, bias, out):
         for b in range(0, BANKS, 2):
             regroup_d2(first + b, nc.scalar.copy)
             regroup_d2(first + b + 1, nc.vector.tensor_copy)
-            quantise_d2(first + b)
-            quantise_d2(first + b + 1)
+            quantise_d2((first + b) // 2)
 
         for half in range(2):
-            term_ps = psum_term.tile([P, M_OUT // 2, J_OUT], F32)
+            term_ps = psum_y.tile([P, M_OUT // 2, J_OUT], F32, tag="y_ps")
             for q in range(M_OUT // 2):
                 m = (M_OUT // 2) * half + q
                 cols = slice(m * T, (m + 1) * T)

@@ -66,10 +66,14 @@ def tile_ttsolver_pa_t_kernel(tc, d1, g1, g2, x_l, mv, bias, out):
         raw_of = {}
         for u in range(UNITS):
             raw = raw_pool.tile([P, PACK, UNIT_COLS], BF16)
-            for half in range(2):
-                cols = slice(half * UNIT_COLS // 2, (half + 1) * UNIT_COLS // 2)
-                start = u * UNIT_COLS + half * UNIT_COLS // 2
-                nc.sync.dma_start(out=raw[:, :, cols], in_=d1_rows[:, :, start : start + UNIT_COLS // 2])
+            pieces = 4 if u == 0 else 1
+            width = UNIT_COLS // pieces
+            for piece in range(pieces):
+                start = u * UNIT_COLS + width * piece
+                nc.sync.dma_start(
+                    out=raw[:, :, width * piece : width * (piece + 1)],
+                    in_=d1_rows[:, :, start : start + width],
+                )
             raw_of[u] = raw
             if u == 0:
                 for h in range(2):

@@ -20,18 +20,16 @@ RANK_B = 16
 J_OUT = 128
 ROW = M_OUT * J_OUT
 
-PAIR = 2
 A_UNIT = 8
 UNITS = A // A_UNIT
 UNIT_COLS = A_UNIT * T
 A_BANK = 4
-Q_BANK = A_BANK // PAIR
-A_LO = 8
+A_LO = 16
 GROUPS = UNITS // PACK
 M_BANK = 2
 BANKS = M_OUT // M_BANK
 RUN = 4
-VECTOR_COLS = 640
+VECTOR_COLS = 656
 TENSOR_COLS = 112
 LAG_BANK = 5
 
@@ -106,23 +104,24 @@ def tile_ttsolver_pa_t_kernel(tc, d1, g1, g2, x_l, mv, bias, out):
                 in_=w1_grouped[:].rearrange("p m s j -> p (m s j)"),
             )
 
-        g2_sorted = keep.tile([P, 2 * GROUPS, A_LO, RANK_B], F32)
+        g2_sorted = keep.tile([P, A, RANK_B], BF16)
         w2_grouped = keep.tile([P, GROUPS, J_OUT, PACK], BF16, align_bytes=64)
         w2_codes = keep.tile([P, GROUPS, J_OUT], U32, align_bytes=64)
         w2_scales = keep.tile([P, GROUPS, J_OUT], U8, align_bytes=64)
 
         def sort_w2():
-            words = g2_raw[:].rearrange("p s a -> p (s a)").bitcast(F32)
             nc.vector.tensor_copy(
-                out=g2_sorted[:], in_=words.rearrange("p (s c a) -> p c a s", s=RANK_B, a=A_LO)
+                out=g2_sorted[:].rearrange("p (c i) s -> p c s i", i=RUN),
+                in_=g2_raw[:].rearrange("p s (c i) -> p c s i", i=RUN),
             )
 
         def transpose_w2(h):
             w_ps = psum_t.tile([P, 2, 2, J_OUT], F32, tag="t_bank")
             for c in range(4):
+                chunk = slice(A_LO * (4 * h + c), A_LO * (4 * h + c + 1))
                 nc.tensor.transpose(
                     w_ps[:, c // 2, c % 2, :],
-                    g2_sorted[:, 4 * h + c, :, :].rearrange("p a s -> p (a s)"),
+                    g2_sorted[:, chunk, :].rearrange("p a s -> p (a s)").bitcast(F32),
                     ident[:],
                 )
             words = w2_grouped[:, 2 * h : 2 * h + 2, :, :].rearrange("p g o j -> p (g o j)").bitcast(F32)
@@ -207,13 +206,13 @@ def tile_ttsolver_pa_t_kernel(tc, d1, g1, g2, x_l, mv, bias, out):
             g = u // PACK
             v = (u // 2) % 2
             if u % PACK == 0:
-                y_group = stage.tile([P, 2, M_OUT, A_LO, RANK_B, PAIR], BF16)
+                y_group = stage.tile([P, 2, M_OUT, A_LO, RANK_B], BF16)
                 y_group_of[g] = y_group
             for b in range(A_UNIT // A_BANK):
-                first = A_UNIT // PAIR * (u % 2) + Q_BANK * b
+                first = A_UNIT * (u % 2) + A_BANK * b
                 nc.scalar.copy(
-                    out=y_group_of[g][:, v, :, first : first + Q_BANK, :, :],
-                    in_=y_banks_of[u][b][:].rearrange("p (q e) (m s) -> p m q s e", e=PAIR, s=RANK_B),
+                    out=y_group_of[g][:, v, :, first : first + A_BANK, :],
+                    in_=y_banks_of[u][b][:].rearrange("p a (m s) -> p m a s", s=RANK_B),
                 )
 
         def transpose_bank(k):
@@ -221,7 +220,7 @@ def tile_ttsolver_pa_t_kernel(tc, d1, g1, g2, x_l, mv, bias, out):
             t_bank = psum_t.tile([P, M_BANK, 2, T], F32)
             for q in range(M_BANK):
                 for v in range(2):
-                    y_words = y_group_of[g][:, v, M_BANK * b + q, :, :, :].rearrange("p a s e -> p (a s e)")
+                    y_words = y_group_of[g][:, v, M_BANK * b + q, :, :].rearrange("p a s -> p (a s)")
                     nc.tensor.transpose(t_bank[:, q, v, :], y_words.bitcast(F32), ident[:])
             t_bank_of[k] = t_bank
 

@@ -29,8 +29,15 @@ GROUPS = UNITS // PACK
 M_BANK = 2
 BANKS = M_OUT // M_BANK
 RUN = 4
-VECTOR_COLS = 656
+VECTOR_COLS = 640
 TENSOR_COLS = 112
+W2_STEP = 7
+MV_STEP = 9
+BIAS_STEP = 11
+W2_CODES_STEP = 13
+EARLY_STEP = 14
+LOAD_UNIT = 6
+EARLY_GROUPS = 2
 LAG_BANK = 5
 
 FLOPS = 2 * 512 * 128 * 16384 + 2 * 2048 * 1024 * 128
@@ -61,6 +68,9 @@ def tile_ttsolver_pa_t_kernel(tc, d1, g1, g2, x_l, mv, bias, out):
 
         g1_raw = keep.tile([P, M_OUT, PACK * RANK_B], BF16)
         g2_raw = keep.tile([P, RANK_B, A], BF16)
+        x_sb = keep.tile([P, ROW], BF16)
+        mv_sb = keep.tile([P, ROW], BF16)
+        bias_sb = keep.tile([P, ROW], BF16)
         raw_of = {}
         for u in range(UNITS):
             raw = raw_pool.tile([P, PACK, UNIT_COLS], BF16)
@@ -73,21 +83,18 @@ def tile_ttsolver_pa_t_kernel(tc, d1, g1, g2, x_l, mv, bias, out):
                     in_=d1_rows[:, :, start : start + width],
                 )
             raw_of[u] = raw
+            if u == LOAD_UNIT:
+                nc.sync.dma_start(out=g2_raw[:], in_=g2.rearrange("s o a x -> o s (a x)"))
+                nc.sync.dma_start(out=x_sb[:], in_=x_rows)
+                nc.sync.dma_start(out=mv_sb[:], in_=mv_rows)
+                for b in range(P // 16):
+                    nc.sync.dma_start(out=bias_sb[16 * b : 16 * (b + 1), :], in_=bias_rows)
             if u == 0:
                 for h in range(2):
                     nc.sync.dma_start(
                         out=g1_raw[h:P:2, :, :],
                         in_=g1[:, :, PACK * h : PACK * (h + 1), :].rearrange("r m j s -> r m (j s)"),
                     )
-        nc.sync.dma_start(out=g2_raw[:], in_=g2.rearrange("s o a x -> o s (a x)"))
-        x_sb = keep.tile([P, ROW], BF16)
-        nc.sync.dma_start(out=x_sb[:], in_=x_rows)
-        mv_sb = keep.tile([P, ROW], BF16)
-        nc.sync.dma_start(out=mv_sb[:], in_=mv_rows)
-        bias_sb = keep.tile([P, ROW], BF16)
-        for b in range(P // 16):
-            nc.sync.dma_start(out=bias_sb[16 * b : 16 * (b + 1), :], in_=bias_rows)
-
         w1_grouped = keep.tile([P, M_OUT, RANK_B, PACK], BF16, align_bytes=64)
         w1_codes = keep.tile([P, M_OUT * RANK_B], U32, align_bytes=64)
         w1_scales = keep.tile([P, M_OUT * RANK_B], U8, align_bytes=64)
@@ -169,19 +176,29 @@ def tile_ttsolver_pa_t_kernel(tc, d1, g1, g2, x_l, mv, bias, out):
                     in_=raw_of[u][:, :, cols].rearrange("p j (c i) -> p c j i", i=RUN),
                 )
 
-            interleave(nc.vector.tensor_copy, slice(0, VECTOR_COLS))
-            interleave(nc.scalar.copy, slice(VECTOR_COLS, UNIT_COLS - TENSOR_COLS))
-            nc.scalar.copy(out=grouped[:, UNIT_COLS - TENSOR_COLS :, :], in_=ordered_of[u][:])
+            if u == 0:
+                quarter = UNIT_COLS // 4
+                interleave(nc.vector.tensor_copy, slice(0, quarter))
+                interleave(nc.scalar.copy, slice(quarter, 2 * quarter))
+                interleave(nc.vector.tensor_copy, slice(2 * quarter, UNIT_COLS))
+            else:
+                interleave(nc.vector.tensor_copy, slice(0, VECTOR_COLS))
+                interleave(nc.scalar.copy, slice(VECTOR_COLS, UNIT_COLS - TENSOR_COLS))
+                nc.scalar.copy(out=grouped[:, UNIT_COLS - TENSOR_COLS :, :], in_=ordered_of[u][:])
             grouped_of[u] = grouped
 
         def quantise_d1(u):
             codes = stage.tile([P, UNIT_COLS], U32, align_bytes=64, bufs=4)
             scales = stage.tile([P, UNIT_COLS], U8, align_bytes=64, bufs=4)
-            nc.vector.quantize_mx(
-                out=codes[:].bitcast(FP8X4),
-                scales=scales[:],
-                in_=grouped_of[u][:].rearrange("p c j -> p (c j)"),
-            )
+            parts = 2 if u == UNITS - 1 else 1
+            width = UNIT_COLS // parts
+            for part in range(parts):
+                cols = slice(width * part, width * (part + 1))
+                nc.vector.quantize_mx(
+                    out=codes[:, cols].bitcast(FP8X4),
+                    scales=scales[:, cols],
+                    in_=grouped_of[u][:, cols, :].rearrange("p c j -> p (c j)"),
+                )
             codes_of[u] = codes
             scales_of[u] = scales
 
@@ -243,10 +260,46 @@ def tile_ttsolver_pa_t_kernel(tc, d1, g1, g2, x_l, mv, bias, out):
                 in_=d2_grouped_of[pair][:].rearrange("p b c j -> p (b c j)"),
             )
 
+        def third_core(term_ps, half, groups):
+            for q in range(M_OUT // 2):
+                m = (M_OUT // 2) * half + q
+                cols = slice(m * T, (m + 1) * T)
+                for g in groups:
+                    nc.tensor.matmul_mx(
+                        out=term_ps[:, q, :],
+                        lhsT=d2_codes[:, g, cols].bitcast(FP8X4),
+                        lhsT_scale=d2_scales[:, g, cols],
+                        rhs=w2_codes[:, g, :].bitcast(FP8X4),
+                        rhs_scale=w2_scales[:, g, :],
+                        start=(g == groups[0]),
+                        stop=(g == groups[-1]),
+                    )
+
+        base = keep.tile([P, ROW], F32)
+        early_of = {}
+
+        def add_mv():
+            nc.vector.tensor_tensor(out=base[:], in0=x_sb[:], in1=mv_sb[:], op=ADD)
+
+        def add_bias():
+            nc.vector.tensor_tensor(out=base[:], in0=base[:], in1=bias_sb[:], op=ADD)
+
+        def early_core(half):
+            early_ps = psum_t.tile([P, M_OUT // 2, J_OUT], F32, tag="t_bank")
+            third_core(early_ps, half, range(EARLY_GROUPS))
+            early_of[half] = early_ps
+
+        def subtract_early(half):
+            cols = slice(half * ROW // 2, (half + 1) * ROW // 2)
+            nc.vector.tensor_tensor(
+                out=base[:, cols],
+                in0=base[:, cols],
+                in1=early_of[half][:].rearrange("p m o -> p (m o)"),
+                op=SUBTRACT,
+            )
+
         for i in range(UNITS + 1):
             k = i - LAG_BANK
-            if i == 0:
-                order_d1(0)
             if i == 1:
                 regroup_w1()
             if i >= 1:
@@ -255,16 +308,26 @@ def tile_ttsolver_pa_t_kernel(tc, d1, g1, g2, x_l, mv, bias, out):
                 quantise_w1()
             if i < UNITS:
                 regroup_d1(i)
-            if i == 11:
+            if i == W2_STEP:
                 sort_w2()
-            if 12 <= i < 14:
-                transpose_w2(i - 12)
-            if i == 14:
+            if W2_STEP < i <= W2_STEP + 2:
+                transpose_w2(i - W2_STEP - 1)
+            if i == W2_CODES_STEP:
                 quantise_w2()
+            if i == MV_STEP:
+                add_mv()
+            if i == BIAS_STEP:
+                add_bias()
+            if i == EARLY_STEP + 1:
+                subtract_early(0)
+                subtract_early(1)
             if k >= 0:
                 transpose_bank(k)
             if i >= 1:
                 second_core(i - 1)
+            if i == EARLY_STEP:
+                early_core(0)
+                early_core(1)
             if i + 1 < UNITS:
                 order_d1(i + 1)
             if k >= 0:
@@ -274,33 +337,17 @@ def tile_ttsolver_pa_t_kernel(tc, d1, g1, g2, x_l, mv, bias, out):
             if k >= 0 and k % 2 == 1:
                 quantise_d2(k // 2)
 
-        base = keep.tile([P, ROW], F32)
-        nc.vector.tensor_tensor(out=base[:], in0=x_sb[:], in1=mv_sb[:], op=ADD)
-        nc.vector.tensor_tensor(out=base[:], in0=base[:], in1=bias_sb[:], op=ADD)
-
         first = (GROUPS - 1) * BANKS
         for b in range(BANKS):
             transpose_bank(first + b)
-        for b in range(0, BANKS, 2):
-            regroup_d2(first + b, nc.scalar.copy)
-            regroup_d2(first + b + 1, nc.vector.tensor_copy)
-            quantise_d2((first + b) // 2)
+        for b in range(BANKS):
+            regroup_d2(first + b, nc.vector.tensor_copy if b == 1 else nc.scalar.copy)
+            if b % 2 == 1:
+                quantise_d2((first + b) // 2)
 
         for half in range(2):
             term_ps = psum_y.tile([P, M_OUT // 2, J_OUT], F32, tag="y_ps")
-            for q in range(M_OUT // 2):
-                m = (M_OUT // 2) * half + q
-                cols = slice(m * T, (m + 1) * T)
-                for g in range(GROUPS):
-                    nc.tensor.matmul_mx(
-                        out=term_ps[:, q, :],
-                        lhsT=d2_codes[:, g, cols].bitcast(FP8X4),
-                        lhsT_scale=d2_scales[:, g, cols],
-                        rhs=w2_codes[:, g, :].bitcast(FP8X4),
-                        rhs_scale=w2_scales[:, g, :],
-                        start=(g == 0),
-                        stop=(g == GROUPS - 1),
-                    )
+            third_core(term_ps, half, range(EARLY_GROUPS, GROUPS))
             cols = slice(half * ROW // 2, (half + 1) * ROW // 2)
             result = stage.tile([P, ROW // 2], F32)
             nc.vector.tensor_tensor(

from contextlib import ExitStack

import concourse.mybir as mybir
from concourse.masks import make_identity

BF16 = mybir.dt.bfloat16
F32 = mybir.dt.float32
U32 = mybir.dt.uint32
U8 = mybir.dt.uint8
FP8X4 = mybir.dt.float8_e4m3fn_x4
ADD = mybir.AluOpType.add
SUBTRACT = mybir.AluOpType.subtract

P = 128
PACK = 4
A = 128
T = 128
M_OUT = 8
RANK_B = 16
J_OUT = 128
ROW = M_OUT * J_OUT

A_UNIT = 8
UNITS = A // A_UNIT
UNIT_COLS = A_UNIT * T
A_BANK = 4
A_LO = 16
GROUPS = UNITS // PACK
M_BANK = 2
BANKS = M_OUT // M_BANK
RUN = 4
VECTOR_COLS = 640
TENSOR_COLS = 112
W2_STEP = 7
MV_STEP = 9
BIAS_STEP = 11
W2_CODES_STEP = 13
EARLY_STEP = 14
LOAD_UNIT = 6
EARLY_GROUPS = 2
LAG_BANK = 5

FLOPS = 2 * 512 * 128 * 16384 + 2 * 2048 * 1024 * 128


def tile_ttsolver_pa_t_kernel(tc, d1, g1, g2, x_l, mv, bias, out):
    nc = tc.nc

    d1_rows = d1.rearrange("r (h j c) t -> (r h) j (c t)", h=2, j=PACK)
    x_rows = x_l.rearrange("b (q c) -> (b q) c", c=ROW)
    mv_rows = mv.rearrange("b (q c) -> (b q) c", c=ROW)
    bias_rows = bias.rearrange("(q c) -> q c", c=ROW)
    out_rows = out.rearrange("b (q c) -> (b q) c", c=ROW)

    with ExitStack() as pools:
        keep = pools.enter_context(tc.tile_pool(name="keep", bufs=1))
        raw_pool = pools.enter_context(tc.tile_pool(name="raw", bufs=12))
        stage = pools.enter_context(tc.tile_pool(name="stage", bufs=2))
        psum_y = pools.enter_context(tc.psum_pool(name="psum_y", bufs=3))
        psum_t = pools.enter_context(tc.psum_pool(name="psum_t", bufs=3))
        psum_d1 = pools.enter_context(tc.psum_pool(name="psum_d1", bufs=2))
        pools.enter_context(tc.manual_schedule())

        ident = keep.tile([P, P], F32)
        make_identity(nc, ident[:])
        ident_bf16 = keep.tile([P, P], BF16)
        make_identity(nc, ident_bf16[:])

        g1_raw = keep.tile([P, M_OUT, PACK * RANK_B], BF16)
        g2_raw = keep.tile([P, RANK_B, A], BF16)
        x_sb = keep.tile([P, ROW], BF16)
        mv_sb = keep.tile([P, ROW], BF16)
        bias_sb = keep.tile([P, ROW], BF16)
        raw_of = {}
        for u in range(UNITS):
            raw = raw_pool.tile([P, PACK, UNIT_COLS], BF16)
            pieces = 4 if u == 0 else 1
            width = UNIT_COLS // pieces
            for piece in range(pieces):
                start = u * UNIT_COLS + width * piece
                nc.sync.dma_start(
                    out=raw[:, :, width * piece : width * (piece + 1)],
                    in_=d1_rows[:, :, start : start + width],
                )
            raw_of[u] = raw
            if u == LOAD_UNIT:
                nc.sync.dma_start(out=g2_raw[:], in_=g2.rearrange("s o a x -> o s (a x)"))
                nc.sync.dma_start(out=x_sb[:], in_=x_rows)
                nc.sync.dma_start(out=mv_sb[:], in_=mv_rows)
                for b in range(P // 16):
                    nc.sync.dma_start(out=bias_sb[16 * b : 16 * (b + 1), :], in_=bias_rows)
            if u == 0:
                for h in range(2):
                    nc.sync.dma_start(
                        out=g1_raw[h:P:2, :, :],
                        in_=g1[:, :, PACK * h : PACK * (h + 1), :].rearrange("r m j s -> r m (j s)"),
                    )
        w1_grouped = keep.tile([P, M_OUT, RANK_B, PACK], BF16, align_bytes=64)
        w1_codes = keep.tile([P, M_OUT * RANK_B], U32, align_bytes=64)
        w1_scales = keep.tile([P, M_OUT * RANK_B], U8, align_bytes=64)

        def regroup_w1():
            nc.vector.tensor_copy(
                out=w1_grouped[:], in_=g1_raw[:].rearrange("p m (j s) -> p m s j", j=PACK)
            )

        def quantise_w1():
            nc.vector.quantize_mx(
                out=w1_codes[:].bitcast(FP8X4),
                scales=w1_scales[:],
                in_=w1_grouped[:].rearrange("p m s j -> p (m s j)"),
            )

        g2_sorted = keep.tile([P, A, RANK_B], BF16)
        w2_grouped = keep.tile([P, GROUPS, J_OUT, PACK], BF16, align_bytes=64)
        w2_codes = keep.tile([P, GROUPS, J_OUT], U32, align_bytes=64)
        w2_scales = keep.tile([P, GROUPS, J_OUT], U8, align_bytes=64)

        def sort_w2():
            nc.vector.tensor_copy(
                out=g2_sorted[:].rearrange("p (c i) s -> p c s i", i=RUN),
                in_=g2_raw[:].rearrange("p s (c i) -> p c s i", i=RUN),
            )

        def transpose_w2(h):
            w_ps = psum_t.tile([P, 2, 2, J_OUT], F32, tag="t_bank")
            for c in range(4):
                chunk = slice(A_LO * (4 * h + c), A_LO * (4 * h + c + 1))
                nc.tensor.transpose(
                    w_ps[:, c // 2, c % 2, :],
                    g2_sorted[:, chunk, :].rearrange("p a s -> p (a s)").bitcast(F32),
                    ident[:],
                )
            words = w2_grouped[:, 2 * h : 2 * h + 2, :, :].rearrange("p g o j -> p (g o j)").bitcast(F32)
            nc.scalar.copy(
                out=words.rearrange("p (g o v) -> p g o v", g=2, v=2),
                in_=w_ps[:].rearrange("p g v o -> p g o v"),
            )

        def quantise_w2():
            nc.vector.quantize_mx(
                out=w2_codes[:].rearrange("p g o -> p (g o)").bitcast(FP8X4),
                scales=w2_scales[:].rearrange("p g o -> p (g o)"),
                in_=w2_grouped[:].rearrange("p g o j -> p (g o j)"),
            )

        d2_codes = keep.tile([P, GROUPS, M_OUT * T], U32, align_bytes=64)
        d2_scales = keep.tile([P, GROUPS, M_OUT * T], U8, align_bytes=64)
        grouped_of = {}
        codes_of = {}
        scales_of = {}
        y_banks_of = {}
        y_group_of = {}
        t_bank_of = {}
        d2_grouped_of = {}

        ordered_of = {}

        def order_d1(u):
            ordered = psum_d1.tile([P, TENSOR_COLS, PACK], BF16)
            nc.tensor.matmul(
                ordered[:],
                lhsT=ident_bf16[:],
                rhs=raw_of[u][:, :, UNIT_COLS - TENSOR_COLS :].rearrange("p j c -> p c j"),
                start=True,
                stop=True,
            )
            ordered_of[u] = ordered

        def regroup_d1(u):
            grouped = stage.tile([P, UNIT_COLS, PACK], BF16, align_bytes=64, bufs=3)

            def interleave(copy, cols):
                copy(
                    out=grouped[:, cols, :].rearrange("p (c i) j -> p c j i", i=RUN),
                    in_=raw_of[u][:, :, cols].rearrange("p j (c i) -> p c j i", i=RUN),
                )

            if u == 0:
                quarter = UNIT_COLS // 4
                interleave(nc.vector.tensor_copy, slice(0, quarter))
                interleave(nc.scalar.copy, slice(quarter, 2 * quarter))
                interleave(nc.vector.tensor_copy, slice(2 * quarter, UNIT_COLS))
            else:
                interleave(nc.vector.tensor_copy, slice(0, VECTOR_COLS))
                interleave(nc.scalar.copy, slice(VECTOR_COLS, UNIT_COLS - TENSOR_COLS))
                nc.scalar.copy(out=grouped[:, UNIT_COLS - TENSOR_COLS :, :], in_=ordered_of[u][:])
            grouped_of[u] = grouped

        def quantise_d1(u):
            codes = stage.tile([P, UNIT_COLS], U32, align_bytes=64, bufs=4)
            scales = stage.tile([P, UNIT_COLS], U8, align_bytes=64, bufs=4)
            parts = 2 if u == UNITS - 1 else 1
            width = UNIT_COLS // parts
            for part in range(parts):
                cols = slice(width * part, width * (part + 1))
                nc.vector.quantize_mx(
                    out=codes[:, cols].bitcast(FP8X4),
                    scales=scales[:, cols],
                    in_=grouped_of[u][:, cols, :].rearrange("p c j -> p (c j)"),
                )
            codes_of[u] = codes
            scales_of[u] = scales

        def second_core(u):
            y_banks_of[u] = []
            for b in range(A_UNIT // A_BANK):
                y_ps = psum_y.tile([P, A_BANK, M_OUT * RANK_B], F32)
                for i in range(A_BANK):
                    cols = slice((A_BANK * b + i) * T, (A_BANK * b + i + 1) * T)
                    nc.tensor.matmul_mx(
                        out=y_ps[:, i, :],
                        lhsT=codes_of[u][:, cols].bitcast(FP8X4),
                        lhsT_scale=scales_of[u][:, cols],
                        rhs=w1_codes[:].bitcast(FP8X4),
                        rhs_scale=w1_scales[:],
                        start=True,
                        stop=True,
                    )
                y_banks_of[u].append(y_ps)

        def round_d2(u):
            g = u // PACK
            v = (u // 2) % 2
            if u % PACK == 0:
                y_group = stage.tile([P, 2, M_OUT, A_LO, RANK_B], BF16)
                y_group_of[g] = y_group
            for b in range(A_UNIT // A_BANK):
                first = A_UNIT * (u % 2) + A_BANK * b
                nc.scalar.copy(
                    out=y_group_of[g][:, v, :, first : first + A_BANK, :],
                    in_=y_banks_of[u][b][:].rearrange("p a (m s) -> p m a s", s=RANK_B),
                )

        def transpose_bank(k):
            g, b = divmod(k, BANKS)
            t_bank = psum_t.tile([P, M_BANK, 2, T], F32)
            for q in range(M_BANK):
                for v in range(2):
                    y_words = y_group_of[g][:, v, M_BANK * b + q, :, :].rearrange("p a s -> p (a s)")
                    nc.tensor.transpose(t_bank[:, q, v, :], y_words.bitcast(F32), ident[:])
            t_bank_of[k] = t_bank

        def regroup_d2(k, copy):
            if k % 2 == 0:
                d2_grouped = stage.tile([P, 2, M_BANK * T, PACK], BF16, align_bytes=64, bufs=3)
                d2_grouped_of[k // 2] = d2_grouped
            words = d2_grouped_of[k // 2][:, k % 2, :, :].rearrange("p c j -> p (c j)").bitcast(F32)
            copy(
                out=words.rearrange("p (q t v) -> p q t v", q=M_BANK, v=2),
                in_=t_bank_of[k][:].rearrange("p q v t -> p q t v"),
            )

        def quantise_d2(pair):
            g, b = divmod(pair, BANKS // 2)
            cols = slice(2 * M_BANK * T * b, 2 * M_BANK * T * (b + 1))
            nc.vector.quantize_mx(
                out=d2_codes[:, g, cols].bitcast(FP8X4),
                scales=d2_scales[:, g, cols],
                in_=d2_grouped_of[pair][:].rearrange("p b c j -> p (b c j)"),
            )

        def third_core(term_ps, half, groups):
            for q in range(M_OUT // 2):
                m = (M_OUT // 2) * half + q
                cols = slice(m * T, (m + 1) * T)
                for g in groups:
                    nc.tensor.matmul_mx(
                        out=term_ps[:, q, :],
                        lhsT=d2_codes[:, g, cols].bitcast(FP8X4),
                        lhsT_scale=d2_scales[:, g, cols],
                        rhs=w2_codes[:, g, :].bitcast(FP8X4),
                        rhs_scale=w2_scales[:, g, :],
                        start=(g == groups[0]),
                        stop=(g == groups[-1]),
                    )

        base = keep.tile([P, ROW], F32)
        early_of = {}

        def add_mv():
            nc.vector.tensor_tensor(out=base[:], in0=x_sb[:], in1=mv_sb[:], op=ADD)

        def add_bias():
            nc.vector.tensor_tensor(out=base[:], in0=base[:], in1=bias_sb[:], op=ADD)

        def early_core(half):
            early_ps = psum_t.tile([P, M_OUT // 2, J_OUT], F32, tag="t_bank")
            third_core(early_ps, half, range(EARLY_GROUPS))
            early_of[half] = early_ps

        def subtract_early(half):
            cols = slice(half * ROW // 2, (half + 1) * ROW // 2)
            nc.vector.tensor_tensor(
                out=base[:, cols],
                in0=base[:, cols],
                in1=early_of[half][:].rearrange("p m o -> p (m o)"),
                op=SUBTRACT,
            )

        for i in range(UNITS + 1):
            k = i - LAG_BANK
            if i == 1:
                regroup_w1()
            if i >= 1:
                quantise_d1(i - 1)
            if i == 1:
                quantise_w1()
            if i < UNITS:
                regroup_d1(i)
            if i == W2_STEP:
                sort_w2()
            if W2_STEP < i <= W2_STEP + 2:
                transpose_w2(i - W2_STEP - 1)
            if i == W2_CODES_STEP:
                quantise_w2()
            if i == MV_STEP:
                add_mv()
            if i == BIAS_STEP:
                add_bias()
            if i == EARLY_STEP + 1:
                subtract_early(0)
                subtract_early(1)
            if k >= 0:
                transpose_bank(k)
            if i >= 1:
                second_core(i - 1)
            if i == EARLY_STEP:
                early_core(0)
                early_core(1)
            if i + 1 < UNITS:
                order_d1(i + 1)
            if k >= 0:
                regroup_d2(k, nc.scalar.copy)
            if i >= 1:
                round_d2(i - 1)
            if k >= 0 and k % 2 == 1:
                quantise_d2(k // 2)

        first = (GROUPS - 1) * BANKS
        for b in range(BANKS):
            transpose_bank(first + b)
        for b in range(BANKS):
            regroup_d2(first + b, nc.vector.tensor_copy if b == 1 else nc.scalar.copy)
            if b % 2 == 1:
                quantise_d2((first + b) // 2)

        for half in range(2):
            term_ps = psum_y.tile([P, M_OUT // 2, J_OUT], F32, tag="y_ps")
            third_core(term_ps, half, range(EARLY_GROUPS, GROUPS))
            cols = slice(half * ROW // 2, (half + 1) * ROW // 2)
            result = stage.tile([P, ROW // 2], F32)
            nc.vector.tensor_tensor(
                out=result[:],
                in0=base[:, cols],
                in1=term_ps[:].rearrange("p m o -> p (m o)"),
                op=SUBTRACT,
            )
            nc.sync.dma_start(out=out_rows[:, cols], in_=result[:])
